import numpy as np
import ml_dtypes


def mxq(x, axis, fmt="e4m3"):
    dtype, down = {"e4m3": (ml_dtypes.float8_e4m3fn, 7), "e5m2": (ml_dtypes.float8_e5m2, 14)}[fmt]
    v = np.moveaxis(np.asarray(x, np.float32).astype(ml_dtypes.bfloat16).astype(np.float64), axis, -1)
    blocks = v.reshape(v.shape[:-1] + (-1, 32))
    amax = np.abs(blocks).max(-1, keepdims=True)
    byte = np.maximum(np.where(amax > 0, np.frexp(amax)[1] - 1 + 127, 0) - down, 1)
    scale = np.exp2(byte - 127.0)
    codes = (blocks / scale).astype(np.float32).astype(dtype).astype(np.float64)
    return np.moveaxis((codes * scale).reshape(v.shape), -1, axis)


WIDE = False


def mx_kscale(k):
    if not WIDE:
        return np.ones(k)
    levels = np.array([10, -10, 5, -5, 0])
    if k % 512:
        return np.exp2(np.random.permutation(np.resize(levels, k // 32))).repeat(32)
    a = np.empty((k // 512, 16))
    for p in range(k // 512):
        a[p, :8] = np.random.permutation(np.resize(levels, 8))
        for g in range(8):
            far = levels[np.abs(levels - a[p, g]) >= 10]
            a[p, g + 8] = far[np.random.randint(len(far))]
    return np.exp2(a.ravel()).repeat(32)


BF16 = ml_dtypes.bfloat16


def bf(x):
    return np.asarray(x, np.float32).astype(BF16)


def f64(x):
    return np.asarray(x).astype(np.float64)


B, CI, CO, N, KM, M = 2, 128, 128, 1024, 32, 512
R = 6.0
A = np.sqrt(R) / N ** 0.25


def setup_inputs():
    u = mx_kscale(CI * KM)[::KM]
    t = mx_kscale(M)
    return {
        "x": bf((np.random.standard_normal((B, CI, N)) + A) * u[None, :, None]),
        "wbases": bf((np.random.standard_normal((B, N, M)) + A) / (R * np.sqrt(N))),
        "bases": bf(np.random.standard_normal((B, N, M)) / np.sqrt(M) / t),
        "weights": bf(np.random.standard_normal((CI, CO, KM)) / np.sqrt(CI * KM) / u[:, None, None]),
        "D": bf(np.random.standard_normal((KM, M)) * t),
    }


def reference(x, wbases, bases, weights, D):
    x_hat = f64(x) @ f64(wbases)[:, :, :M]
    z = (x_hat[:, :, None, :] * f64(D)[None, None, :, :]).reshape(B, CI * KM, M)
    w2 = f64(weights).transpose(0, 2, 1).reshape(CI * KM, CO)
    y_hat = mxq(w2, 0, "e4m3").T @ mxq(z, 1, "e4m3")
    return mxq(y_hat, 2, "e4m3") @ mxq(f64(bases)[:, :, :M], 2, "e4m3").transpose(0, 2, 1)

@@ -1,0 +1,291 @@
+from contextlib import ExitStack
+
+import concourse.mybir as mybir
+from concourse.masks import make_identity
+
+F32 = mybir.dt.float32
+BF16 = mybir.dt.bfloat16
+U32 = mybir.dt.uint32
+U8 = mybir.dt.uint8
+FP8X4 = mybir.dt.float8_e4m3fn_x4
+MULT = mybir.AluOpType.mult
+
+NB, CI, CO, NPTS, KM, NM = 2, 128, 128, 1024, 32, 512
+P = 128
+NG = NPTS // P
+NKC = NM // P
+NC = CI * KM // 512
+NU = NB * NKC
+AV = 92
+AG = P - AV
+FLOPS = 2 * NB * (CI * NPTS * NM + CI * KM * CO * NM + CO * NM * NPTS)
+
+
+def tile_phydgalerkinconv_kernel(tc, x, wbases, bases, weights, D, out):
+    nc = tc.nc
+    with ExitStack() as ctx:
+        keep = ctx.enter_context(tc.tile_pool(name="keep", bufs=1))
+        work = ctx.enter_context(tc.tile_pool(name="work", bufs=2))
+        psum = ctx.enter_context(tc.psum_pool(name="psum", bufs=2))
+        ctx.enter_context(tc.manual_schedule())
+
+        ident_b = keep.tile([P, P], BF16, name="ident_b")
+        make_identity(nc, ident_b[:])
+        ident_f = keep.tile([P, P], F32, name="ident_f")
+        make_identity(nc, ident_f[:])
+
+        warm_in = keep.tile([P, 512], BF16, name="warm_in")
+        nc.vector.memset(warm_in[:], 0.0)
+        warm_ps = psum.tile([P, 512], F32, tag="xr", bufs=4, name="warm_ps")
+        for w in range(4):
+            nc.tensor.matmul(out=warm_ps[:], lhsT=warm_in[:, 0:P], rhs=warm_in[:], start=True, stop=True)
+
+        x_sb = [keep.tile([P, NPTS], BF16, name="x_sb%d" % b) for b in range(NB)]
+        wb_sb = [keep.tile([P, NG, NM], BF16, name="wb_sb%d" % b) for b in range(NB)]
+        bs_sb = [keep.tile([P, NG * NM], BF16, name="bs_sb%d" % b) for b in range(NB)]
+        d_load = keep.tile([P, 4 * NM], BF16, name="d_load")
+        w_om = keep.tile([P, CI * KM], BF16, name="w_om")
+
+        def load_d(r):
+            nc.sync.dma_start(
+                out=d_load[r:P:8, :],
+                in_=D[4 * r:4 * r + 4, :].rearrange("t k -> (t k)").partition_broadcast(16),
+            )
+
+        wb0 = wbases[0].rearrange("(g p) k -> p g k", p=P)
+        load_d(0)
+        load_d(1)
+        nc.sync.dma_start(out=x_sb[0][:], in_=x[0])
+        nc.sync.dma_start(out=wb_sb[0][:, 0:4, :], in_=wb0[:, 0:4, :])
+        nc.sync.dma_start(out=wb_sb[0][:, 4:8, :], in_=wb0[:, 4:8, :])
+        for r in range(2, 8):
+            load_d(r)
+
+        nc.sync.dma_start(out=x_sb[1][:], in_=x[1])
+        nc.sync.dma_start(out=wb_sb[1][:], in_=wbases[1].rearrange("(g p) k -> p g k", p=P))
+        def load_bases(b):
+            nc.sync.dma_start(
+                out=bs_sb[b][:].rearrange("p (g k) -> p g k", g=NG),
+                in_=bases[b].rearrange("(g p) k -> p g k", p=P),
+            )
+
+        load_bases(0)
+        for q in range(4):
+            nc.sync.dma_start(
+                out=w_om[:, 1024 * q:1024 * (q + 1)].rearrange("o (i j) -> o i j", j=KM),
+                in_=weights[32 * q:32 * (q + 1)].rearrange("i o j -> o i j"),
+            )
+        load_bases(1)
+
+        x_t = [keep.tile([P, NG, CI], BF16, name="x_t%d" % b) for b in range(NB)]
+
+        def transpose_x(b, half):
+            xt_ps = psum.tile([P, 4, CI], BF16, tag="aux", name="xt_ps")
+            for gg in range(4):
+                g = 4 * half + gg
+                nc.tensor.transpose(xt_ps[:, gg, :], x_sb[b][:, g * P:(g + 1) * P], ident_b[:])
+            if b == 0 and half == 0:
+                nc.vector.tensor_copy(out=x_t[b][:, 4 * half:4 * half + 4, :], in_=xt_ps[:])
+            else:
+                nc.scalar.copy(out=x_t[b][:, 4 * half:4 * half + 4, :], in_=xt_ps[:])
+
+        d_rep = keep.tile([P, NKC, P, 4], BF16, name="d_rep")
+
+        def regroup_d(u):
+            view = d_load[:].rearrange("p (t q e) -> p e q t", t=4, e=4)
+            if u == 0:
+                nc.vector.tensor_copy(out=d_rep[:, 0:2, :, :], in_=view[:, 0:2])
+            else:
+                nc.scalar.copy(out=d_rep[:, 2:4, :, :], in_=view[:, 2:4])
+
+        w_grp = keep.tile([P, NC * CO * 4], BF16, name="w_grp", align_bytes=64)
+        w_code = keep.tile([P, NC * CO], U32, name="w_code", align_bytes=64)
+        w_scale = keep.tile([P, NC * CO], U8, name="w_scale", align_bytes=64)
+
+        def transpose_weights(cp):
+            words = w_om[:].bitcast(F32).rearrange("o (c p u) -> o c p u", c=NC, u=2)
+            grp_words = w_grp[:].bitcast(F32).rearrange("p (c o u) -> p c o u", c=NC, u=2)
+            wt_ps = psum.tile([P, 2, 2, CO], F32, tag="aux", name="wt_ps")
+            for cc in range(2):
+                for u in range(2):
+                    nc.tensor.transpose(wt_ps[:, cc, u, :], words[:, 2 * cp + cc, :, u], ident_f[:])
+            nc.scalar.copy(
+                out=grp_words[:, 2 * cp:2 * cp + 2, :, :],
+                in_=wt_ps[:].rearrange("p c u o -> p c o u"),
+            )
+
+        def quantise_weights():
+            nc.vector.quantize_mx(out=w_code[:].bitcast(FP8X4), scales=w_scale[:], in_=w_grp[:])
+
+        b_grp = [keep.tile([P, NPTS * 4], BF16, name="b_grp%d" % b, align_bytes=64) for b in range(NB)]
+        b_code = [keep.tile([P, NPTS], U32, name="b_code%d" % b, align_bytes=64) for b in range(NB)]
+        b_scale = [keep.tile([P, NPTS], U8, name="b_scale%d" % b, align_bytes=64) for b in range(NB)]
+
+        def transpose_bases(b, gp):
+            words = bs_sb[b][:].bitcast(F32).rearrange("p (g w u) -> p g u w", g=NG, u=2)
+            grp_words = b_grp[b][:].bitcast(F32).rearrange("p (g n u) -> p g n u", g=NG, u=2)
+            bt_ps = psum.tile([P, 2, 2, P], F32, tag="aux", name="bt_ps")
+            for gg in range(2):
+                for u in range(2):
+                    nc.tensor.transpose(bt_ps[:, gg, u, :], words[:, 2 * gp + gg, u, :], ident_f[:])
+            nc.scalar.copy(
+                out=grp_words[:, 2 * gp:2 * gp + 2, :, :],
+                in_=bt_ps[:].rearrange("p g u n -> p g n u"),
+            )
+
+        def quantise_bases(b):
+            nc.vector.quantize_mx(out=b_code[b][:].bitcast(FP8X4), scales=b_scale[b][:], in_=b_grp[b][:])
+
+        z_code = [keep.tile([P, NC * P], U32, name="z_code%d" % n, align_bytes=64) for n in range(NU)]
+        z_scale = [keep.tile([P, NC * P], U8, name="z_scale%d" % n, align_bytes=64) for n in range(NU)]
+        xh = {}
+        rep = {}
+        xr = {}
+        xg = {}
+        z = {}
+        y_t = {}
+
+        def project(n):
+            b, kc = divmod(n, NKC)
+            wbv = wb_sb[b][:].rearrange("p g (q e) -> p g e q", e=NKC)
+            xh[n] = psum.tile([P, CI], F32, tag="acc", name="xh")
+            for g in range(NG):
+                nc.tensor.matmul(
+                    out=xh[n][:], lhsT=wbv[:, g, kc, :], rhs=x_t[b][:, g, :],
+                    start=(g == 0), stop=(g == NG - 1),
+                )
+
+        def replicate(n):
+            rep[n] = work.tile([P, CI * 8], F32, tag="rep", bufs=3, name="rep")
+            for h in range(2):
+                nc.scalar.copy(
+                    out=rep[n][:, 512 * h:512 * (h + 1)].rearrange("k (i r) -> k i r", r=8),
+                    in_=xh[n][:, 64 * h:64 * (h + 1)].unsqueeze(2).to_broadcast([P, 64, 8]),
+                )
+
+        def spread(n, h):
+            xr[n, h] = psum.tile([P, 4, P], F32, tag="xr", bufs=4, name="xr")
+            for cc in range(4):
+                c = 4 * h + cc
+                nc.tensor.transpose(xr[n, h][:, cc, :], rep[n][:, c * P:(c + 1) * P], ident_f[:])
+            if h == 0:
+                xg[n] = work.tile([P, NC, AG], F32, tag="xg", bufs=3, name="xg")
+            nc.scalar.copy(out=xg[n][:, 4 * h:4 * h + 4, :], in_=xr[n, h][:, :, AV:P])
+
+        def multiply(n):
+            kc = n % NKC
+            z[n] = work.tile([P, NC * P * 4], BF16, tag="z", name="z", align_bytes=64)
+            zv = z[n][:].rearrange("p (c k t) -> p c k t", c=NC, t=4)
+            nc.gpsimd.tensor_tensor(
+                out=zv[:, :, AV:P, :],
+                in0=xg[n][:].unsqueeze(3).to_broadcast([P, NC, AG, 4]),
+                in1=d_rep[:, kc, AV:P, :].unsqueeze(1).to_broadcast([P, NC, AG, 4]),
+                op=MULT,
+            )
+            for h in range(2):
+                nc.vector.tensor_tensor(
+                    out=zv[:, 4 * h:4 * h + 4, 0:AV, :],
+                    in0=xr[n, h][:, :, 0:AV].unsqueeze(3).to_broadcast([P, 4, AV, 4]),
+                    in1=d_rep[:, kc, 0:AV, :].unsqueeze(1).to_broadcast([P, 4, AV, 4]),
+                    op=MULT,
+                )
+
+        def quantise(n, pieces):
+            wide = NC * P // pieces
+            for s in range(pieces):
+                nc.vector.quantize_mx(
+                    out=z_code[n][:, wide * s:wide * (s + 1)].bitcast(FP8X4),
+                    scales=z_scale[n][:, wide * s:wide * (s + 1)],
+                    in_=z[n][:, 4 * wide * s:4 * wide * (s + 1)],
+                )
+
+        def contract(n):
+            b, kc = divmod(n, NKC)
+            if kc == 0:
+                y_t[b] = psum.tile([P, NKC, CO], F32, tag="acc", name="y_t")
+            for c in range(NC):
+                nc.tensor.matmul_mx(
+                    out=y_t[b][:, kc, :],
+                    lhsT=z_code[n][:, c * P:(c + 1) * P].bitcast(FP8X4), lhsT_scale=z_scale[n][:, c * P:(c + 1) * P],
+                    rhs=w_code[:, c * CO:(c + 1) * CO].bitcast(FP8X4), rhs_scale=w_scale[:, c * CO:(c + 1) * CO],
+                    start=(c == 0), stop=(c == NC - 1),
+                )
+
+        yg = {}
+        yc = {}
+        ys = {}
+
+        def round_y(b):
+            yg[b] = work.tile([P, CO * 4], BF16, tag="yg", name="yg", align_bytes=64)
+            nc.scalar.copy(out=yg[b][:].rearrange("p (o t) -> p o t", t=4), in_=y_t[b][:].rearrange("p t o -> p o t"))
+
+        def quantise_y(b):
+            yc[b] = work.tile([P, CO], U32, tag="yc", name="yc", align_bytes=64)
+            ys[b] = work.tile([P, CO], U8, tag="ys", name="ys", align_bytes=64)
+            nc.vector.quantize_mx(out=yc[b][:].bitcast(FP8X4), scales=ys[b][:], in_=yg[b][:])
+
+        def reconstruct(b):
+            for nh in range(2):
+                yp = psum.tile([P, 512], F32, tag="aux", name="yp")
+                nc.tensor.matmul_mx(
+                    out=yp[:], lhsT=yc[b][:].bitcast(FP8X4), lhsT_scale=ys[b][:],
+                    rhs=b_code[b][:, 512 * nh:512 * (nh + 1)].bitcast(FP8X4),
+                    rhs_scale=b_scale[b][:, 512 * nh:512 * (nh + 1)],
+                    start=True, stop=True,
+                )
+                yo = work.tile([P, 512], F32, tag="yo", bufs=4, name="yo")
+                if b == NB - 1 and nh == 0:
+                    nc.vector.tensor_copy(out=yo[:], in_=yp[:])
+                else:
+                    nc.scalar.copy(out=yo[:], in_=yp[:])
+                nc.sync.dma_start(out=out[b][:, 512 * nh:512 * (nh + 1)], in_=yo[:])
+
+        side_jobs = [(transpose_x, (1, 0)), (transpose_x, (1, 1))]
+        side_jobs.extend([(transpose_bases, (0, gp)) for gp in range(4)])
+        side_jobs.extend([(transpose_weights, (cp,)) for cp in range(4)])
+        side_jobs.extend([(transpose_bases, (1, gp)) for gp in range(4)])
+
+        transpose_x(0, 0)
+        transpose_x(0, 1)
+        regroup_d(0)
+        project(0)
+        replicate(0)
+        project(1)
+        for r in range(NU):
+            spread(r, 0)
+            if r < 2:
+                spread(r, 1)
+            if r + 2 < NU:
+                project(r + 2)
+            if r >= 2:
+                spread(r, 1)
+            if r + 1 < NU:
+                replicate(r + 1)
+            if r == 0:
+                regroup_d(1)
+            if r >= 1:
+                for job, arguments in side_jobs[2 * r - 2:2 * r]:
+                    job(*arguments)
+            if r == NU - 1:
+                for n in range(NKC):
+                    contract(n)
+                round_y(0)
+                for n in range(NKC, NU - 2):
+                    contract(n)
+            multiply(r)
+            if r == NU - 1:
+                quantise_y(0)
+                reconstruct(0)
+            if r >= 1:
+                quantise(r - 1, 1)
+            if r == 3:
+                quantise_bases(0)
+            if r == 5:
+                quantise_weights()
+        quantise(NU - 1, 2)
+        contract(NU - 2)
+        contract(NU - 1)
+        round_y(1)
+        quantise_bases(1)
+        quantise_y(1)
+        reconstruct(1)

@@ -16,8 +16,8 @@ NG = NPTS // P
 NKC = NM // P
 NC = CI * KM // 512
 NU = NB * NKC
-AV = 92
-AG = P - AV
+AG = 72
+AV = P - AG
 FLOPS = 2 * NB * (CI * NPTS * NM + CI * KM * CO * NM + CO * NM * NPTS)
 
 
@@ -168,25 +168,26 @@ def tile_phydgalerkinconv_kernel(tc, x, wbases, bases, weights, D, out):
             for cc in range(4):
                 c = 4 * h + cc
                 nc.tensor.transpose(xr[n, h][:, cc, :], rep[n][:, c * P:(c + 1) * P], ident_f[:])
-            if h == 0:
-                xg[n] = work.tile([P, NC, AG], F32, tag="xg", bufs=3, name="xg")
-            nc.scalar.copy(out=xg[n][:, 4 * h:4 * h + 4, :], in_=xr[n, h][:, :, AV:P])
+            if h == 1:
+                xg[n] = work.tile([P, 4, AG], F32, tag="xg", bufs=3, name="xg")
+                nc.scalar.copy(out=xg[n][:], in_=xr[n, h][:, :, AV:P])
 
         def multiply(n):
             kc = n % NKC
             z[n] = work.tile([P, NC * P * 4], BF16, tag="z", name="z", align_bytes=64)
             zv = z[n][:].rearrange("p (c k t) -> p c k t", c=NC, t=4)
             nc.gpsimd.tensor_tensor(
-                out=zv[:, :, AV:P, :],
-                in0=xg[n][:].unsqueeze(3).to_broadcast([P, NC, AG, 4]),
-                in1=d_rep[:, kc, AV:P, :].unsqueeze(1).to_broadcast([P, NC, AG, 4]),
+                out=zv[:, 4:NC, AV:P, :],
+                in0=xg[n][:].unsqueeze(3).to_broadcast([P, 4, AG, 4]),
+                in1=d_rep[:, kc, AV:P, :].unsqueeze(1).to_broadcast([P, 4, AG, 4]),
                 op=MULT,
             )
             for h in range(2):
+                width = P if h == 0 else AV
                 nc.vector.tensor_tensor(
-                    out=zv[:, 4 * h:4 * h + 4, 0:AV, :],
-                    in0=xr[n, h][:, :, 0:AV].unsqueeze(3).to_broadcast([P, 4, AV, 4]),
-                    in1=d_rep[:, kc, 0:AV, :].unsqueeze(1).to_broadcast([P, 4, AV, 4]),
+                    out=zv[:, 4 * h:4 * h + 4, 0:width, :],
+                    in0=xr[n, h][:, :, 0:width].unsqueeze(3).to_broadcast([P, 4, width, 4]),
+                    in1=d_rep[:, kc, 0:width, :].unsqueeze(1).to_broadcast([P, 4, width, 4]),
                     op=MULT,
                 )
 

@@ -34,35 +34,34 @@ def tile_phydgalerkinconv_kernel(tc, x, wbases, bases, weights, D, out):
         ident_f = keep.tile([P, P], F32, name="ident_f")
         make_identity(nc, ident_f[:])
 
-        warm_in = keep.tile([P, 512], BF16, name="warm_in")
-        nc.vector.memset(warm_in[:], 0.0)
-        warm_ps = psum.tile([P, 512], F32, tag="xr", bufs=4, name="warm_ps")
-        for w in range(4):
-            nc.tensor.matmul(out=warm_ps[:], lhsT=warm_in[:, 0:P], rhs=warm_in[:], start=True, stop=True)
+        warm_in = keep.tile([P, 4 * P], BF16, name="warm_in", align_bytes=64)
+        warm_code = keep.tile([P, P], U32, name="warm_code", align_bytes=64)
+        warm_scale = keep.tile([P, P], U8, name="warm_scale", align_bytes=64)
+        nc.vector.memset(warm_in[:].bitcast(F32), 0.0)
+        nc.vector.quantize_mx(out=warm_code[:].bitcast(FP8X4), scales=warm_scale[:], in_=warm_in[:])
+        warm_ps = psum.tile([P, P], F32, tag="xr", bufs=4, name="warm_ps")
+        for w in range(8):
+            nc.tensor.matmul_mx(
+                out=warm_ps[:], lhsT=warm_code[:].bitcast(FP8X4), lhsT_scale=warm_scale[:],
+                rhs=warm_code[:].bitcast(FP8X4), rhs_scale=warm_scale[:], start=True, stop=True,
+            )
 
         x_sb = [keep.tile([P, NPTS], BF16, name="x_sb%d" % b) for b in range(NB)]
         wb_sb = [keep.tile([P, NG, NM], BF16, name="wb_sb%d" % b) for b in range(NB)]
         bs_sb = [keep.tile([P, NG * NM], BF16, name="bs_sb%d" % b) for b in range(NB)]
-        d_load = keep.tile([P, 4 * NM], BF16, name="d_load")
+        d_pad = keep.tile([P, NM], BF16, name="d_pad")
+        nc.vector.memset(d_pad[32:64, :].bitcast(F32), 0.0)
+        nc.vector.memset(d_pad[64:P, :].bitcast(F32), 0.0)
         w_om = keep.tile([P, CI * KM], BF16, name="w_om")
 
-        def load_d(r):
-            nc.sync.dma_start(
-                out=d_load[r:P:8, :],
-                in_=D[4 * r:4 * r + 4, :].rearrange("t k -> (t k)").partition_broadcast(16),
-            )
-
         wb0 = wbases[0].rearrange("(g p) k -> p g k", p=P)
-        load_d(0)
-        load_d(1)
+        nc.sync.dma_start(out=d_pad[0:KM, :], in_=D[:, :])
         nc.sync.dma_start(out=x_sb[0][:], in_=x[0])
-        nc.sync.dma_start(out=wb_sb[0][:, 0:4, :], in_=wb0[:, 0:4, :])
-        nc.sync.dma_start(out=wb_sb[0][:, 4:8, :], in_=wb0[:, 4:8, :])
-        for r in range(2, 8):
-            load_d(r)
-
+        nc.sync.dma_start(out=wb_sb[0][:, :, 0:256], in_=wb0[:, :, 0:256])
+        nc.sync.dma_start(out=wb_sb[0][:, :, 256:512], in_=wb0[:, :, 256:512])
         nc.sync.dma_start(out=x_sb[1][:], in_=x[1])
         nc.sync.dma_start(out=wb_sb[1][:], in_=wbases[1].rearrange("(g p) k -> p g k", p=P))
+
         def load_bases(b):
             nc.sync.dma_start(
                 out=bs_sb[b][:].rearrange("p (g k) -> p g k", g=NG),
@@ -89,14 +88,30 @@ def tile_phydgalerkinconv_kernel(tc, x, wbases, bases, weights, D, out):
             else:
                 nc.scalar.copy(out=x_t[b][:, 4 * half:4 * half + 4, :], in_=xt_ps[:])
 
-        d_rep = keep.tile([P, NKC, P, 4], BF16, name="d_rep")
+        selector = keep.tile([P, 4, P], BF16, name="selector")
+        nc.vector.tensor_copy(
+            out=selector[:].rearrange("j t (i r) -> j t i r", r=8),
+            in_=ident_b[:, 0:KM].rearrange("j (r t) -> j t r", t=4).unsqueeze(2).to_broadcast([P, 4, 16, 8]),
+        )
+        d_rep = keep.tile([P, NM, 4], BF16, name="d_rep")
 
-        def regroup_d(u):
-            view = d_load[:].rearrange("p (t q e) -> p e q t", t=4, e=4)
-            if u == 0:
-                nc.vector.tensor_copy(out=d_rep[:, 0:2, :, :], in_=view[:, 0:2])
+        def replicate_d(q):
+            if q < 2:
+                dr_ps = psum.tile([P, 4, P], F32, tag="xr", bufs=4, name="dr_ps")
             else:
-                nc.scalar.copy(out=d_rep[:, 2:4, :, :], in_=view[:, 2:4])
+                dr_ps = psum.tile([P, 4, P], F32, tag="aux", name="dr_ps")
+            for t in range(4):
+                nc.tensor.matmul(
+                    out=dr_ps[:, t, :], lhsT=selector[:, t, :], rhs=d_pad[:, P * q:P * (q + 1)], start=True, stop=True,
+                )
+            copy = nc.vector.tensor_copy if q < 2 else nc.scalar.copy
+            copy(out=d_rep[:, P * q:P * (q + 1), :], in_=dr_ps[:].rearrange("p t m -> p m t"))
+
+        def d_modes(n, first, last):
+            b, kc = divmod(n, NKC)
+            if b == 0:
+                return d_rep[:, P * kc + first:P * kc + last, :]
+            return d_rep[:].rearrange("p (q e) t -> p e q t", e=NKC)[:, kc, first:last, :]
 
         w_grp = keep.tile([P, NC * CO * 4], BF16, name="w_grp", align_bytes=64)
         w_code = keep.tile([P, NC * CO], U32, name="w_code", align_bytes=64)
@@ -145,9 +160,13 @@ def tile_phydgalerkinconv_kernel(tc, x, wbases, bases, weights, D, out):
         z = {}
         y_t = {}
 
+        def parts(n):
+            return [(0, 2), (2, 2), (4, 4)] if n == 0 else [(0, 4), (4, 4)]
+
         def project(n):
             b, kc = divmod(n, NKC)
-            wbv = wb_sb[b][:].rearrange("p g (q e) -> p g e q", e=NKC)
+            pattern = "p g (e q) -> p g e q" if b == 0 else "p g (q e) -> p g e q"
+            wbv = wb_sb[b][:].rearrange(pattern, e=NKC)
             xh[n] = psum.tile([P, CI], F32, tag="acc", name="xh")
             for g in range(NG):
                 nc.tensor.matmul(
@@ -157,37 +176,37 @@ def tile_phydgalerkinconv_kernel(tc, x, wbases, bases, weights, D, out):
 
         def replicate(n):
             rep[n] = work.tile([P, CI * 8], F32, tag="rep", bufs=3, name="rep")
-            for h in range(2):
+            for c, count in parts(n):
                 nc.scalar.copy(
-                    out=rep[n][:, 512 * h:512 * (h + 1)].rearrange("k (i r) -> k i r", r=8),
-                    in_=xh[n][:, 64 * h:64 * (h + 1)].unsqueeze(2).to_broadcast([P, 64, 8]),
+                    out=rep[n][:, P * c:P * (c + count)].rearrange("k (i r) -> k i r", r=8),
+                    in_=xh[n][:, 16 * c:16 * (c + count)].unsqueeze(2).to_broadcast([P, 16 * count, 8]),
                 )
 
         def spread(n, h):
-            xr[n, h] = psum.tile([P, 4, P], F32, tag="xr", bufs=4, name="xr")
-            for cc in range(4):
-                c = 4 * h + cc
+            first, count = parts(n)[h]
+            xr[n, h] = psum.tile([P, count, P], F32, tag="xr", bufs=4, name="xr")
+            for cc in range(count):
+                c = first + cc
                 nc.tensor.transpose(xr[n, h][:, cc, :], rep[n][:, c * P:(c + 1) * P], ident_f[:])
-            if h == 1:
+            if first == 4:
                 xg[n] = work.tile([P, 4, AG], F32, tag="xg", bufs=3, name="xg")
                 nc.scalar.copy(out=xg[n][:], in_=xr[n, h][:, :, AV:P])
 
         def multiply(n):
-            kc = n % NKC
             z[n] = work.tile([P, NC * P * 4], BF16, tag="z", name="z", align_bytes=64)
             zv = z[n][:].rearrange("p (c k t) -> p c k t", c=NC, t=4)
             nc.gpsimd.tensor_tensor(
                 out=zv[:, 4:NC, AV:P, :],
                 in0=xg[n][:].unsqueeze(3).to_broadcast([P, 4, AG, 4]),
-                in1=d_rep[:, kc, AV:P, :].unsqueeze(1).to_broadcast([P, 4, AG, 4]),
+                in1=d_modes(n, AV, P).unsqueeze(1).to_broadcast([P, 4, AG, 4]),
                 op=MULT,
             )
-            for h in range(2):
-                width = P if h == 0 else AV
+            for h, (first, count) in enumerate(parts(n)):
+                width = P if first < 4 else AV
                 nc.vector.tensor_tensor(
-                    out=zv[:, 4 * h:4 * h + 4, 0:width, :],
-                    in0=xr[n, h][:, :, 0:width].unsqueeze(3).to_broadcast([P, 4, width, 4]),
-                    in1=d_rep[:, kc, 0:width, :].unsqueeze(1).to_broadcast([P, 4, width, 4]),
+                    out=zv[:, first:first + count, 0:width, :],
+                    in0=xr[n, h][:, :, 0:width].unsqueeze(3).to_broadcast([P, count, width, 4]),
+                    in1=d_modes(n, 0, width).unsqueeze(1).to_broadcast([P, count, width, 4]),
                     op=MULT,
                 )
 
@@ -205,10 +224,12 @@ def tile_phydgalerkinconv_kernel(tc, x, wbases, bases, weights, D, out):
             if kc == 0:
                 y_t[b] = psum.tile([P, NKC, CO], F32, tag="acc", name="y_t")
             for c in range(NC):
+                z_op = z_code[n][:, c * P:(c + 1) * P].bitcast(FP8X4), z_scale[n][:, c * P:(c + 1) * P]
+                w_op = w_code[:, c * CO:(c + 1) * CO].bitcast(FP8X4), w_scale[:, c * CO:(c + 1) * CO]
+                stationary, moving = (w_op, z_op) if b == 0 else (z_op, w_op)
                 nc.tensor.matmul_mx(
                     out=y_t[b][:, kc, :],
-                    lhsT=z_code[n][:, c * P:(c + 1) * P].bitcast(FP8X4), lhsT_scale=z_scale[n][:, c * P:(c + 1) * P],
-                    rhs=w_code[:, c * CO:(c + 1) * CO].bitcast(FP8X4), rhs_scale=w_scale[:, c * CO:(c + 1) * CO],
+                    lhsT=stationary[0], lhsT_scale=stationary[1], rhs=moving[0], rhs_scale=moving[1],
                     start=(c == 0), stop=(c == NC - 1),
                 )
 
@@ -218,7 +239,20 @@ def tile_phydgalerkinconv_kernel(tc, x, wbases, bases, weights, D, out):
 
         def round_y(b):
             yg[b] = work.tile([P, CO * 4], BF16, tag="yg", name="yg", align_bytes=64)
-            nc.scalar.copy(out=yg[b][:].rearrange("p (o t) -> p o t", t=4), in_=y_t[b][:].rearrange("p t o -> p o t"))
+            if b == 0:
+                y_om = work.tile([P, NM], BF16, name="y_om", align_bytes=64)
+                nc.scalar.copy(out=y_om[:], in_=y_t[b][:].rearrange("o e m -> o (e m)"))
+                words = y_om[:].bitcast(F32).rearrange("o (p u) -> o p u", u=2)
+                yt_ps = psum.tile([P, 2, CO], F32, tag="aux", name="yt_ps")
+                for u in range(2):
+                    nc.tensor.transpose(yt_ps[:, u, :], words[:, :, u], ident_f[:])
+                nc.scalar.copy(
+                    out=yg[b][:].bitcast(F32).rearrange("p (o u) -> p o u", u=2), in_=yt_ps[:].rearrange("p u o -> p o u"),
+                )
+            else:
+                nc.scalar.copy(
+                    out=yg[b][:].rearrange("p (o t) -> p o t", t=4), in_=y_t[b][:].rearrange("p t o -> p o t"),
+                )
 
         def quantise_y(b):
             yc[b] = work.tile([P, CO], U32, tag="yc", name="yc", align_bytes=64)
@@ -246,15 +280,21 @@ def tile_phydgalerkinconv_kernel(tc, x, wbases, bases, weights, D, out):
         side_jobs.extend([(transpose_weights, (cp,)) for cp in range(4)])
         side_jobs.extend([(transpose_bases, (1, gp)) for gp in range(4)])
 
+        replicate_d(0)
         transpose_x(0, 0)
         transpose_x(0, 1)
-        regroup_d(0)
+        replicate_d(1)
         project(0)
         replicate(0)
+        spread(0, 0)
         project(1)
         for r in range(NU):
-            spread(r, 0)
-            if r < 2:
+            if r == 0:
+                spread(0, 1)
+                spread(0, 2)
+            else:
+                spread(r, 0)
+            if r == 1:
                 spread(r, 1)
             if r + 2 < NU:
                 project(r + 2)
@@ -263,7 +303,9 @@ def tile_phydgalerkinconv_kernel(tc, x, wbases, bases, weights, D, out):
             if r + 1 < NU:
                 replicate(r + 1)
             if r == 0:
-                regroup_d(1)
+                replicate_d(2)
+            if r == 1:
+                replicate_d(3)
             if r >= 1:
                 for job, arguments in side_jobs[2 * r - 2:2 * r]:
                     job(*arguments)

@@ -16,7 +16,7 @@ NG = NPTS // P
 NKC = NM // P
 NC = CI * KM // 512
 NU = NB * NKC
-AG = 72
+AG = 80
 AV = P - AG
 FLOPS = 2 * NB * (CI * NPTS * NM + CI * KM * CO * NM + CO * NM * NPTS)
 

@@ -9,6 +9,7 @@ U32 = mybir.dt.uint32
 U8 = mybir.dt.uint8
 FP8X4 = mybir.dt.float8_e4m3fn_x4
 MULT = mybir.AluOpType.mult
+COPY = mybir.ActivationFunctionType.Copy
 
 NB, CI, CO, NPTS, KM, NM = 2, 128, 128, 1024, 32, 512
 P = 128
@@ -16,8 +17,8 @@ NG = NPTS // P
 NKC = NM // P
 NC = CI * KM // 512
 NU = NB * NKC
-AG = 80
-AV = P - AG
+SU = NKC - 1
+AG_FIRST, AG_HALF, AG = 48, 36, 76
 FLOPS = 2 * NB * (CI * NPTS * NM + CI * KM * CO * NM + CO * NM * NPTS)
 
 
@@ -29,6 +30,9 @@ def tile_phydgalerkinconv_kernel(tc, x, wbases, bases, weights, D, out):
         psum = ctx.enter_context(tc.psum_pool(name="psum", bufs=2))
         ctx.enter_context(tc.manual_schedule())
 
+        d_pad = keep.tile([P, NM], BF16, name="d_pad")
+        nc.vector.memset(d_pad[32:64, :].bitcast(F32), 0.0)
+        nc.vector.memset(d_pad[64:P, :].bitcast(F32), 0.0)
         ident_b = keep.tile([P, P], BF16, name="ident_b")
         make_identity(nc, ident_b[:])
         ident_f = keep.tile([P, P], F32, name="ident_f")
@@ -49,9 +53,6 @@ def tile_phydgalerkinconv_kernel(tc, x, wbases, bases, weights, D, out):
         x_sb = [keep.tile([P, NPTS], BF16, name="x_sb%d" % b) for b in range(NB)]
         wb_sb = [keep.tile([P, NG, NM], BF16, name="wb_sb%d" % b) for b in range(NB)]
         bs_sb = [keep.tile([P, NG * NM], BF16, name="bs_sb%d" % b) for b in range(NB)]
-        d_pad = keep.tile([P, NM], BF16, name="d_pad")
-        nc.vector.memset(d_pad[32:64, :].bitcast(F32), 0.0)
-        nc.vector.memset(d_pad[64:P, :].bitcast(F32), 0.0)
         w_om = keep.tile([P, CI * KM], BF16, name="w_om")
 
         wb0 = wbases[0].rearrange("(g p) k -> p g k", p=P)
@@ -68,12 +69,12 @@ def tile_phydgalerkinconv_kernel(tc, x, wbases, bases, weights, D, out):
                 in_=bases[b].rearrange("(g p) k -> p g k", p=P),
             )
 
-        load_bases(0)
         for q in range(4):
             nc.sync.dma_start(
                 out=w_om[:, 1024 * q:1024 * (q + 1)].rearrange("o (i j) -> o i j", j=KM),
                 in_=weights[32 * q:32 * (q + 1)].rearrange("i o j -> o i j"),
             )
+        load_bases(0)
         load_bases(1)
 
         x_t = [keep.tile([P, NG, CI], BF16, name="x_t%d" % b) for b in range(NB)]
@@ -117,9 +118,9 @@ def tile_phydgalerkinconv_kernel(tc, x, wbases, bases, weights, D, out):
         w_code = keep.tile([P, NC * CO], U32, name="w_code", align_bytes=64)
         w_scale = keep.tile([P, NC * CO], U8, name="w_scale", align_bytes=64)
 
-        def transpose_weights(cp):
-            words = w_om[:].bitcast(F32).rearrange("o (c p u) -> o c p u", c=NC, u=2)
-            grp_words = w_grp[:].bitcast(F32).rearrange("p (c o u) -> p c o u", c=NC, u=2)
+        def turn_words(source, target, cp):
+            words = source[:].bitcast(F32).rearrange("o (c p u) -> o c p u", p=P, u=2)
+            grp_words = target[:].bitcast(F32).rearrange("p (c o u) -> p c o u", c=NC, u=2)
             wt_ps = psum.tile([P, 2, 2, CO], F32, tag="aux", name="wt_ps")
             for cc in range(2):
                 for u in range(2):
@@ -128,6 +129,9 @@ def tile_phydgalerkinconv_kernel(tc, x, wbases, bases, weights, D, out):
                 out=grp_words[:, 2 * cp:2 * cp + 2, :, :],
                 in_=wt_ps[:].rearrange("p c u o -> p c o u"),
             )
+
+        def transpose_weights(cp):
+            turn_words(w_om, w_grp, cp)
 
         def quantise_weights():
             nc.vector.quantize_mx(out=w_code[:].bitcast(FP8X4), scales=w_scale[:], in_=w_grp[:])
@@ -160,8 +164,13 @@ def tile_phydgalerkinconv_kernel(tc, x, wbases, bases, weights, D, out):
         z = {}
         y_t = {}
 
+        def share(n):
+            return AG_FIRST if n == 0 else AG_HALF if n == SU else AG
+
         def parts(n):
-            return [(0, 2), (2, 2), (4, 4)] if n == 0 else [(0, 4), (4, 4)]
+            if n == 0:
+                return [(0, 2), (2, 2), (4, 4)]
+            return [(4, 4)] if n == SU else [(4, 4), (0, 4)]
 
         def project(n):
             b, kc = divmod(n, NKC)
@@ -189,26 +198,45 @@ def tile_phydgalerkinconv_kernel(tc, x, wbases, bases, weights, D, out):
                 c = first + cc
                 nc.tensor.transpose(xr[n, h][:, cc, :], rep[n][:, c * P:(c + 1) * P], ident_f[:])
             if first == 4:
-                xg[n] = work.tile([P, 4, AG], F32, tag="xg", bufs=3, name="xg")
-                nc.scalar.copy(out=xg[n][:], in_=xr[n, h][:, :, AV:P])
+                xg[n] = work.tile([P, 4, share(n)], F32, tag="xg", bufs=3, name="xg")
+                nc.scalar.copy(out=xg[n][:], in_=xr[n, h][:, :, P - share(n):P])
 
         def multiply(n):
             z[n] = work.tile([P, NC * P * 4], BF16, tag="z", name="z", align_bytes=64)
             zv = z[n][:].rearrange("p (c k t) -> p c k t", c=NC, t=4)
             nc.gpsimd.tensor_tensor(
-                out=zv[:, 4:NC, AV:P, :],
-                in0=xg[n][:].unsqueeze(3).to_broadcast([P, 4, AG, 4]),
-                in1=d_modes(n, AV, P).unsqueeze(1).to_broadcast([P, 4, AG, 4]),
+                out=zv[:, 4:NC, P - share(n):P, :],
+                in0=xg[n][:].unsqueeze(3).to_broadcast([P, 4, share(n), 4]),
+                in1=d_modes(n, P - share(n), P).unsqueeze(1).to_broadcast([P, 4, share(n), 4]),
                 op=MULT,
             )
             for h, (first, count) in enumerate(parts(n)):
-                width = P if first < 4 else AV
+                width = P if first < 4 else P - share(n)
                 nc.vector.tensor_tensor(
                     out=zv[:, first:first + count, 0:width, :],
                     in0=xr[n, h][:, :, 0:width].unsqueeze(3).to_broadcast([P, count, width, 4]),
                     in1=d_modes(n, 0, width).unsqueeze(1).to_broadcast([P, count, width, 4]),
                     op=MULT,
                 )
+
+        d_t = keep.tile([P, KM], BF16, name="d_t")
+        x_su = keep.tile([P, CI // 2], F32, name="x_su")
+        z_km = keep.tile([P, CI // 2 * KM], BF16, name="z_km")
+
+        def transpose_d():
+            dt_ps = psum.tile([P, P], BF16, tag="aux", name="dt_ps")
+            nc.tensor.transpose(dt_ps[:], d_pad[:, P * SU:P * (SU + 1)], ident_b[:])
+            nc.scalar.copy(out=d_t[:], in_=dt_ps[:, 0:KM])
+
+        def keep_x():
+            nc.scalar.copy(out=x_su[:], in_=xh[SU][:, 0:CI // 2])
+
+        def scale_d(part):
+            for i in range(16 * part, 16 * (part + 1)):
+                nc.scalar.activation(out=z_km[:, KM * i:KM * (i + 1)], in_=d_t[:], func=COPY, scale=x_su[:, i:i + 1])
+
+        def turn_z(cp):
+            turn_words(z_km, z[SU], cp)
 
         def quantise(n, pieces):
             wide = NC * P // pieces
@@ -233,6 +261,7 @@ def tile_phydgalerkinconv_kernel(tc, x, wbases, bases, weights, D, out):
                     start=(c == 0), stop=(c == NC - 1),
                 )
 
+        y_om = keep.tile([P, NM], BF16, name="y_om", align_bytes=64)
         yg = {}
         yc = {}
         ys = {}
@@ -240,19 +269,20 @@ def tile_phydgalerkinconv_kernel(tc, x, wbases, bases, weights, D, out):
         def round_y(b):
             yg[b] = work.tile([P, CO * 4], BF16, tag="yg", name="yg", align_bytes=64)
             if b == 0:
-                y_om = work.tile([P, NM], BF16, name="y_om", align_bytes=64)
                 nc.scalar.copy(out=y_om[:], in_=y_t[b][:].rearrange("o e m -> o (e m)"))
-                words = y_om[:].bitcast(F32).rearrange("o (p u) -> o p u", u=2)
-                yt_ps = psum.tile([P, 2, CO], F32, tag="aux", name="yt_ps")
-                for u in range(2):
-                    nc.tensor.transpose(yt_ps[:, u, :], words[:, :, u], ident_f[:])
-                nc.scalar.copy(
-                    out=yg[b][:].bitcast(F32).rearrange("p (o u) -> p o u", u=2), in_=yt_ps[:].rearrange("p u o -> p o u"),
-                )
             else:
                 nc.scalar.copy(
                     out=yg[b][:].rearrange("p (o t) -> p o t", t=4), in_=y_t[b][:].rearrange("p t o -> p o t"),
                 )
+
+        def turn_y(b):
+            words = y_om[:].bitcast(F32).rearrange("o (p u) -> o p u", u=2)
+            yt_ps = psum.tile([P, 2, CO], F32, tag="aux", name="yt_ps")
+            for u in range(2):
+                nc.tensor.transpose(yt_ps[:, u, :], words[:, :, u], ident_f[:])
+            nc.scalar.copy(
+                out=yg[b][:].bitcast(F32).rearrange("p (o u) -> p o u", u=2), in_=yt_ps[:].rearrange("p u o -> p o u"),
+            )
 
         def quantise_y(b):
             yc[b] = work.tile([P, CO], U32, tag="yc", name="yc", align_bytes=64)
@@ -261,24 +291,31 @@ def tile_phydgalerkinconv_kernel(tc, x, wbases, bases, weights, D, out):
 
         def reconstruct(b):
             for nh in range(2):
-                yp = psum.tile([P, 512], F32, tag="aux", name="yp")
-                nc.tensor.matmul_mx(
-                    out=yp[:], lhsT=yc[b][:].bitcast(FP8X4), lhsT_scale=ys[b][:],
-                    rhs=b_code[b][:, 512 * nh:512 * (nh + 1)].bitcast(FP8X4),
-                    rhs_scale=b_scale[b][:, 512 * nh:512 * (nh + 1)],
-                    start=True, stop=True,
-                )
                 yo = work.tile([P, 512], F32, tag="yo", bufs=4, name="yo")
-                if b == NB - 1 and nh == 0:
-                    nc.vector.tensor_copy(out=yo[:], in_=yp[:])
-                else:
-                    nc.scalar.copy(out=yo[:], in_=yp[:])
+                pieces = 1 if b == 0 else 2
+                wide = 512 // pieces
+                for piece in range(pieces):
+                    first = 512 * nh + wide * piece
+                    yp = psum.tile([P, wide], F32, tag="xr", bufs=4, name="yp")
+                    nc.tensor.matmul_mx(
+                        out=yp[:], lhsT=yc[b][:].bitcast(FP8X4), lhsT_scale=ys[b][:],
+                        rhs=b_code[b][:, first:first + wide].bitcast(FP8X4), rhs_scale=b_scale[b][:, first:first + wide],
+                        start=True, stop=True,
+                    )
+                    copy = nc.vector.tensor_copy if b == 1 and piece == 0 else nc.scalar.copy
+                    copy(out=yo[:, wide * piece:wide * (piece + 1)], in_=yp[:])
                 nc.sync.dma_start(out=out[b][:, 512 * nh:512 * (nh + 1)], in_=yo[:])
 
-        side_jobs = [(transpose_x, (1, 0)), (transpose_x, (1, 1))]
-        side_jobs.extend([(transpose_bases, (0, gp)) for gp in range(4)])
-        side_jobs.extend([(transpose_weights, (cp,)) for cp in range(4)])
-        side_jobs.extend([(transpose_bases, (1, gp)) for gp in range(4)])
+        side_jobs = [
+            [],
+            [(replicate_d, (2,)), (replicate_d, (3,)), (transpose_d, ())],
+            [(scale_d, (0,)), (scale_d, (1,)), (transpose_weights, (0,))],
+            [(scale_d, (2,)), (scale_d, (3,)), (transpose_weights, (1,))],
+            [(turn_z, (0,)), (turn_z, (1,)), (transpose_weights, (2,)), (transpose_weights, (3,))],
+            [(transpose_bases, (0, gp)) for gp in range(3)],
+            [(transpose_bases, (0, 3)), (transpose_bases, (1, 0)), (transpose_bases, (1, 1)), (contract, (0,))],
+            [(contract, (1,)), (contract, (2,)), (transpose_bases, (1, 2)), (transpose_bases, (1, 3)), (contract, (SU,)), (round_y, (0,)), (contract, (SU + 1,))],
+        ]
 
         replicate_d(0)
         transpose_x(0, 0)
@@ -292,43 +329,35 @@ def tile_phydgalerkinconv_kernel(tc, x, wbases, bases, weights, D, out):
             if r == 0:
                 spread(0, 1)
                 spread(0, 2)
-            else:
-                spread(r, 0)
-            if r == 1:
+            elif r != SU:
                 spread(r, 1)
+            if r == 1:
+                transpose_x(1, 0)
+                transpose_x(1, 1)
             if r + 2 < NU:
                 project(r + 2)
-            if r >= 2:
-                spread(r, 1)
             if r + 1 < NU:
                 replicate(r + 1)
-            if r == 0:
-                replicate_d(2)
-            if r == 1:
-                replicate_d(3)
-            if r >= 1:
-                for job, arguments in side_jobs[2 * r - 2:2 * r]:
-                    job(*arguments)
-            if r == NU - 1:
-                for n in range(NKC):
-                    contract(n)
-                round_y(0)
-                for n in range(NKC, NU - 2):
-                    contract(n)
+            if r + 1 == SU:
+                keep_x()
+            if r + 1 < NU:
+                spread(r + 1, 0)
+            for job, arguments in side_jobs[r]:
+                job(*arguments)
             multiply(r)
-            if r == NU - 1:
-                quantise_y(0)
-                reconstruct(0)
-            if r >= 1:
-                quantise(r - 1, 1)
-            if r == 3:
-                quantise_bases(0)
             if r == 5:
                 quantise_weights()
+            if r >= 1:
+                quantise(r - 1, 1)
+        turn_y(0)
+        contract(NU - 3)
         quantise(NU - 1, 2)
         contract(NU - 2)
         contract(NU - 1)
         round_y(1)
+        quantise_bases(0)
+        quantise_y(0)
+        reconstruct(0)
         quantise_bases(1)
         quantise_y(1)
         reconstruct(1)

@@ -31,8 +31,6 @@ def tile_phydgalerkinconv_kernel(tc, x, wbases, bases, weights, D, out):
         ctx.enter_context(tc.manual_schedule())
 
         d_pad = keep.tile([P, NM], BF16, name="d_pad")
-        nc.vector.memset(d_pad[32:64, :].bitcast(F32), 0.0)
-        nc.vector.memset(d_pad[64:P, :].bitcast(F32), 0.0)
         ident_b = keep.tile([P, P], BF16, name="ident_b")
         make_identity(nc, ident_b[:])
         ident_f = keep.tile([P, P], F32, name="ident_f")
@@ -43,6 +41,8 @@ def tile_phydgalerkinconv_kernel(tc, x, wbases, bases, weights, D, out):
         warm_scale = keep.tile([P, P], U8, name="warm_scale", align_bytes=64)
         nc.vector.memset(warm_in[:].bitcast(F32), 0.0)
         nc.vector.quantize_mx(out=warm_code[:].bitcast(FP8X4), scales=warm_scale[:], in_=warm_in[:])
+        nc.vector.memset(d_pad[32:64, :].bitcast(F32), 0.0)
+        nc.vector.memset(d_pad[64:P, :].bitcast(F32), 0.0)
         warm_ps = psum.tile([P, P], F32, tag="xr", bufs=4, name="warm_ps")
         for w in range(8):
             nc.tensor.matmul_mx(
@@ -56,9 +56,10 @@ def tile_phydgalerkinconv_kernel(tc, x, wbases, bases, weights, D, out):
         w_om = keep.tile([P, CI * KM], BF16, name="w_om")
 
         wb0 = wbases[0].rearrange("(g p) k -> p g k", p=P)
-        nc.sync.dma_start(out=d_pad[0:KM, :], in_=D[:, :])
         nc.sync.dma_start(out=x_sb[0][:], in_=x[0])
-        nc.sync.dma_start(out=wb_sb[0][:, :, 0:256], in_=wb0[:, :, 0:256])
+        nc.sync.dma_start(out=d_pad[0:KM, :], in_=D[:, :])
+        nc.sync.dma_start(out=wb_sb[0][:, :, 0:128], in_=wb0[:, :, 0:128])
+        nc.sync.dma_start(out=wb_sb[0][:, :, 128:256], in_=wb0[:, :, 128:256])
         nc.sync.dma_start(out=wb_sb[0][:, :, 256:512], in_=wb0[:, :, 256:512])
         nc.sync.dma_start(out=x_sb[1][:], in_=x[1])
         nc.sync.dma_start(out=wb_sb[1][:], in_=wbases[1].rearrange("(g p) k -> p g k", p=P))
@@ -84,7 +85,7 @@ def tile_phydgalerkinconv_kernel(tc, x, wbases, bases, weights, D, out):
             for gg in range(4):
                 g = 4 * half + gg
                 nc.tensor.transpose(xt_ps[:, gg, :], x_sb[b][:, g * P:(g + 1) * P], ident_b[:])
-            if b == 0 and half == 0:
+            if b == 0:
                 nc.vector.tensor_copy(out=x_t[b][:, 4 * half:4 * half + 4, :], in_=xt_ps[:])
             else:
                 nc.scalar.copy(out=x_t[b][:, 4 * half:4 * half + 4, :], in_=xt_ps[:])
@@ -306,20 +307,30 @@ def tile_phydgalerkinconv_kernel(tc, x, wbases, bases, weights, D, out):
                     copy(out=yo[:, wide * piece:wide * (piece + 1)], in_=yp[:])
                 nc.sync.dma_start(out=out[b][:, 512 * nh:512 * (nh + 1)], in_=yo[:])
 
-        side_jobs = [
+        early_jobs = [
+            [],
+            [],
+            [(scale_d, (0,))],
+            [(scale_d, (2,))],
+            [(turn_z, (0,)), (turn_z, (1,))],
+            [(transpose_bases, (0, 0))],
+            [(transpose_bases, (0, 3))],
+            [],
+        ]
+        late_jobs = [
             [],
             [(replicate_d, (2,)), (replicate_d, (3,)), (transpose_d, ())],
-            [(scale_d, (0,)), (scale_d, (1,)), (transpose_weights, (0,))],
-            [(scale_d, (2,)), (scale_d, (3,)), (transpose_weights, (1,))],
-            [(turn_z, (0,)), (turn_z, (1,)), (transpose_weights, (2,)), (transpose_weights, (3,))],
-            [(transpose_bases, (0, gp)) for gp in range(3)],
-            [(transpose_bases, (0, 3)), (transpose_bases, (1, 0)), (transpose_bases, (1, 1)), (contract, (0,))],
+            [(scale_d, (1,)), (transpose_weights, (0,))],
+            [(scale_d, (3,)), (transpose_weights, (1,))],
+            [(transpose_weights, (2,)), (transpose_weights, (3,))],
+            [(transpose_bases, (0, 1)), (transpose_bases, (0, 2))],
+            [(transpose_bases, (1, 0)), (transpose_bases, (1, 1)), (contract, (0,))],
             [(contract, (1,)), (contract, (2,)), (transpose_bases, (1, 2)), (transpose_bases, (1, 3)), (contract, (SU,)), (round_y, (0,)), (contract, (SU + 1,))],
         ]
 
-        replicate_d(0)
         transpose_x(0, 0)
         transpose_x(0, 1)
+        replicate_d(0)
         replicate_d(1)
         project(0)
         replicate(0)
@@ -340,9 +351,11 @@ def tile_phydgalerkinconv_kernel(tc, x, wbases, bases, weights, D, out):
                 replicate(r + 1)
             if r + 1 == SU:
                 keep_x()
+            for job, arguments in early_jobs[r]:
+                job(*arguments)
             if r + 1 < NU:
                 spread(r + 1, 0)
-            for job, arguments in side_jobs[r]:
+            for job, arguments in late_jobs[r]:
                 job(*arguments)
             multiply(r)
             if r == 5:

@@ -17,7 +17,7 @@ NG = NPTS // P
 NKC = NM // P
 NC = CI * KM // 512
 NU = NB * NKC
-SU = NKC - 1
+HALF = (NKC - 1,)
 AG_FIRST, AG_HALF, AG = 48, 36, 76
 FLOPS = 2 * NB * (CI * NPTS * NM + CI * KM * CO * NM + CO * NM * NPTS)
 
@@ -44,7 +44,7 @@ def tile_phydgalerkinconv_kernel(tc, x, wbases, bases, weights, D, out):
         nc.vector.memset(d_pad[32:64, :].bitcast(F32), 0.0)
         nc.vector.memset(d_pad[64:P, :].bitcast(F32), 0.0)
         warm_ps = psum.tile([P, P], F32, tag="xr", bufs=4, name="warm_ps")
-        for w in range(8):
+        for w in range(12):
             nc.tensor.matmul_mx(
                 out=warm_ps[:], lhsT=warm_code[:].bitcast(FP8X4), lhsT_scale=warm_scale[:],
                 rhs=warm_code[:].bitcast(FP8X4), rhs_scale=warm_scale[:], start=True, stop=True,
@@ -153,8 +153,10 @@ def tile_phydgalerkinconv_kernel(tc, x, wbases, bases, weights, D, out):
                 in_=bt_ps[:].rearrange("p g u n -> p g n u"),
             )
 
-        def quantise_bases(b):
-            nc.vector.quantize_mx(out=b_code[b][:].bitcast(FP8X4), scales=b_scale[b][:], in_=b_grp[b][:])
+        def quantise_bases(b, first, last):
+            nc.vector.quantize_mx(
+                out=b_code[b][:, first:last].bitcast(FP8X4), scales=b_scale[b][:, first:last], in_=b_grp[b][:, 4 * first:4 * last],
+            )
 
         z_code = [keep.tile([P, NC * P], U32, name="z_code%d" % n, align_bytes=64) for n in range(NU)]
         z_scale = [keep.tile([P, NC * P], U8, name="z_scale%d" % n, align_bytes=64) for n in range(NU)]
@@ -166,12 +168,12 @@ def tile_phydgalerkinconv_kernel(tc, x, wbases, bases, weights, D, out):
         y_t = {}
 
         def share(n):
-            return AG_FIRST if n == 0 else AG_HALF if n == SU else AG
+            return AG_FIRST if n == 0 else AG_HALF if n in HALF else AG
 
         def parts(n):
             if n == 0:
                 return [(0, 2), (2, 2), (4, 4)]
-            return [(4, 4)] if n == SU else [(4, 4), (0, 4)]
+            return [(4, 4)] if n in HALF else [(4, 4), (0, 4)]
 
         def project(n):
             b, kc = divmod(n, NKC)
@@ -203,7 +205,8 @@ def tile_phydgalerkinconv_kernel(tc, x, wbases, bases, weights, D, out):
                 nc.scalar.copy(out=xg[n][:], in_=xr[n, h][:, :, P - share(n):P])
 
         def multiply(n):
-            z[n] = work.tile([P, NC * P * 4], BF16, tag="z", name="z", align_bytes=64)
+            if n not in HALF:
+                z[n] = work.tile([P, NC * P * 4], BF16, tag="z", name="z", align_bytes=64)
             zv = z[n][:].rearrange("p (c k t) -> p c k t", c=NC, t=4)
             nc.gpsimd.tensor_tensor(
                 out=zv[:, 4:NC, P - share(n):P, :],
@@ -220,24 +223,30 @@ def tile_phydgalerkinconv_kernel(tc, x, wbases, bases, weights, D, out):
                     op=MULT,
                 )
 
-        d_t = keep.tile([P, KM], BF16, name="d_t")
-        x_su = keep.tile([P, CI // 2], F32, name="x_su")
-        z_km = keep.tile([P, CI // 2 * KM], BF16, name="z_km")
+        d_t = {n: keep.tile([P, KM], BF16, name="d_t%d" % n) for n in HALF}
+        x_half = {n: keep.tile([P, CI // 2], F32, name="x_half%d" % n) for n in HALF}
+        for n in HALF:
+            z[n] = keep.tile([P, NC * P * 4], BF16, name="z_half%d" % n, align_bytes=64)
+        z_km = {n: keep.tile([P, CI // 2 * KM], BF16, name="z_km%d" % n) for n in HALF}
 
-        def transpose_d():
+        def transpose_d(n):
+            b, kc = divmod(n, NKC)
+            modes = d_pad[:, P * kc:P * (kc + 1)] if b == 0 else d_pad[:, kc:NM:NKC]
             dt_ps = psum.tile([P, P], BF16, tag="aux", name="dt_ps")
-            nc.tensor.transpose(dt_ps[:], d_pad[:, P * SU:P * (SU + 1)], ident_b[:])
-            nc.scalar.copy(out=d_t[:], in_=dt_ps[:, 0:KM])
+            nc.tensor.transpose(dt_ps[:], modes, ident_b[:])
+            nc.scalar.copy(out=d_t[n][:], in_=dt_ps[:, 0:KM])
 
-        def keep_x():
-            nc.scalar.copy(out=x_su[:], in_=xh[SU][:, 0:CI // 2])
+        def keep_x(n):
+            nc.scalar.copy(out=x_half[n][:], in_=xh[n][:, 0:CI // 2])
 
-        def scale_d(part):
+        def scale_d(n, part):
             for i in range(16 * part, 16 * (part + 1)):
-                nc.scalar.activation(out=z_km[:, KM * i:KM * (i + 1)], in_=d_t[:], func=COPY, scale=x_su[:, i:i + 1])
+                nc.scalar.activation(
+                    out=z_km[n][:, KM * i:KM * (i + 1)], in_=d_t[n][:], func=COPY, scale=x_half[n][:, i:i + 1],
+                )
 
-        def turn_z(cp):
-            turn_words(z_km, z[SU], cp)
+        def turn_z(n, cp):
+            turn_words(z_km[n], z[n], cp)
 
         def quantise(n, pieces):
             wide = NC * P // pieces
@@ -267,13 +276,15 @@ def tile_phydgalerkinconv_kernel(tc, x, wbases, bases, weights, D, out):
         yc = {}
         ys = {}
 
-        def round_y(b):
-            yg[b] = work.tile([P, CO * 4], BF16, tag="yg", name="yg", align_bytes=64)
+        def round_y(b, first, last):
+            if first == 0:
+                yg[b] = work.tile([P, CO * 4], BF16, tag="yg", name="yg", align_bytes=64)
             if b == 0:
                 nc.scalar.copy(out=y_om[:], in_=y_t[b][:].rearrange("o e m -> o (e m)"))
             else:
                 nc.scalar.copy(
-                    out=yg[b][:].rearrange("p (o t) -> p o t", t=4), in_=y_t[b][:].rearrange("p t o -> p o t"),
+                    out=yg[b][:].rearrange("p (o t) -> p o t", t=4)[:, :, first:last],
+                    in_=y_t[b][:, first:last, :].rearrange("p t o -> p o t"),
                 )
 
         def turn_y(b):
@@ -290,42 +301,50 @@ def tile_phydgalerkinconv_kernel(tc, x, wbases, bases, weights, D, out):
             ys[b] = work.tile([P, CO], U8, tag="ys", name="ys", align_bytes=64)
             nc.vector.quantize_mx(out=yc[b][:].bitcast(FP8X4), scales=ys[b][:], in_=yg[b][:])
 
-        def reconstruct(b):
-            for nh in range(2):
-                yo = work.tile([P, 512], F32, tag="yo", bufs=4, name="yo")
-                pieces = 1 if b == 0 else 2
-                wide = 512 // pieces
-                for piece in range(pieces):
-                    first = 512 * nh + wide * piece
-                    yp = psum.tile([P, wide], F32, tag="xr", bufs=4, name="yp")
-                    nc.tensor.matmul_mx(
-                        out=yp[:], lhsT=yc[b][:].bitcast(FP8X4), lhsT_scale=ys[b][:],
-                        rhs=b_code[b][:, first:first + wide].bitcast(FP8X4), rhs_scale=b_scale[b][:, first:first + wide],
-                        start=True, stop=True,
-                    )
-                    copy = nc.vector.tensor_copy if b == 1 and piece == 0 else nc.scalar.copy
-                    copy(out=yo[:, wide * piece:wide * (piece + 1)], in_=yp[:])
-                nc.sync.dma_start(out=out[b][:, 512 * nh:512 * (nh + 1)], in_=yo[:])
+        def reconstruct(b, nh):
+            yo = work.tile([P, 512], F32, tag="yo", bufs=4, name="yo")
+            copies = [nc.vector.tensor_copy, nc.scalar.copy] if b == NB - 1 and nh == 1 else [nc.scalar.copy]
+            wide = 512 // len(copies)
+            for piece, copy in enumerate(copies):
+                first = 512 * nh + wide * piece
+                yp = psum.tile([P, wide], F32, tag="xr", bufs=4, name="yp")
+                nc.tensor.matmul_mx(
+                    out=yp[:], lhsT=yc[b][:].bitcast(FP8X4), lhsT_scale=ys[b][:],
+                    rhs=b_code[b][:, first:first + wide].bitcast(FP8X4), rhs_scale=b_scale[b][:, first:first + wide],
+                    start=True, stop=True,
+                )
+                copy(out=yo[:, wide * piece:wide * (piece + 1)], in_=yp[:])
+            nc.sync.dma_start(out=out[b][:, 512 * nh:512 * (nh + 1)], in_=yo[:])
 
         early_jobs = [
             [],
             [],
-            [(scale_d, (0,))],
-            [(scale_d, (2,))],
-            [(turn_z, (0,)), (turn_z, (1,))],
+            [(scale_d, (3, 0))],
+            [(scale_d, (3, 2))],
+            [(turn_z, (3, 0)), (turn_z, (3, 1))],
             [(transpose_bases, (0, 0))],
             [(transpose_bases, (0, 3))],
             [],
         ]
         late_jobs = [
             [],
-            [(replicate_d, (2,)), (replicate_d, (3,)), (transpose_d, ())],
-            [(scale_d, (1,)), (transpose_weights, (0,))],
-            [(scale_d, (3,)), (transpose_weights, (1,))],
+            [(replicate_d, (2,)), (replicate_d, (3,)), (transpose_d, (3,))],
+            [(scale_d, (3, 1)), (transpose_weights, (0,))],
+            [(scale_d, (3, 3)), (transpose_weights, (1,))],
             [(transpose_weights, (2,)), (transpose_weights, (3,))],
             [(transpose_bases, (0, 1)), (transpose_bases, (0, 2))],
             [(transpose_bases, (1, 0)), (transpose_bases, (1, 1)), (contract, (0,))],
-            [(contract, (1,)), (contract, (2,)), (transpose_bases, (1, 2)), (transpose_bases, (1, 3)), (contract, (SU,)), (round_y, (0,)), (contract, (SU + 1,))],
+            [(contract, (1,)), (contract, (2,)), (transpose_bases, (1, 2)), (transpose_bases, (1, 3)), (contract, (3,)), (round_y, (0, 0, 4)), (contract, (3 + 1,))],
+        ]
+        quantises = [
+            [],
+            [(quantise, (0, 1))],
+            [],
+            [(quantise, (1, 1))],
+            [(quantise, (2, 1))],
+            [(quantise_weights, ()), (quantise, (3, 1)), (quantise, (4, 1))],
+            [(quantise, (5, 1))],
+            [(quantise, (6, 1))],
         ]
 
         transpose_x(0, 0)
@@ -340,7 +359,7 @@ def tile_phydgalerkinconv_kernel(tc, x, wbases, bases, weights, D, out):
             if r == 0:
                 spread(0, 1)
                 spread(0, 2)
-            elif r != SU:
+            elif r not in HALF:
                 spread(r, 1)
             if r == 1:
                 transpose_x(1, 0)
@@ -349,8 +368,8 @@ def tile_phydgalerkinconv_kernel(tc, x, wbases, bases, weights, D, out):
                 project(r + 2)
             if r + 1 < NU:
                 replicate(r + 1)
-            if r + 1 == SU:
-                keep_x()
+            if r + 1 in HALF:
+                keep_x(r + 1)
             for job, arguments in early_jobs[r]:
                 job(*arguments)
             if r + 1 < NU:
@@ -358,19 +377,22 @@ def tile_phydgalerkinconv_kernel(tc, x, wbases, bases, weights, D, out):
             for job, arguments in late_jobs[r]:
                 job(*arguments)
             multiply(r)
-            if r == 5:
-                quantise_weights()
-            if r >= 1:
-                quantise(r - 1, 1)
+            for job, arguments in quantises[r]:
+                job(*arguments)
         turn_y(0)
         contract(NU - 3)
-        quantise(NU - 1, 2)
+        round_y(1, 0, 2)
         contract(NU - 2)
-        contract(NU - 1)
-        round_y(1)
-        quantise_bases(0)
+        quantise_bases(0, 0, 512)
         quantise_y(0)
-        reconstruct(0)
-        quantise_bases(1)
+        reconstruct(0, 0)
+        quantise(NU - 1, 4)
+        contract(NU - 1)
+        round_y(1, 2, 4)
+        quantise_bases(0, 512, NPTS)
+        reconstruct(0, 1)
+        quantise_bases(1, 0, 512)
         quantise_y(1)
-        reconstruct(1)
+        reconstruct(1, 0)
+        quantise_bases(1, 512, NPTS)
+        reconstruct(1, 1)

@@ -18,7 +18,7 @@ NKC = NM // P
 NC = CI * KM // 512
 NU = NB * NKC
 HALF = (NKC - 1,)
-AG_FIRST, AG_HALF, AG = 48, 36, 76
+AG_FIRST, AG_HALF, AG = 56, 36, 76
 FLOPS = 2 * NB * (CI * NPTS * NM + CI * KM * CO * NM + CO * NM * NPTS)
 
 
@@ -57,8 +57,8 @@ def tile_phydgalerkinconv_kernel(tc, x, wbases, bases, weights, D, out):
 
         wb0 = wbases[0].rearrange("(g p) k -> p g k", p=P)
         nc.sync.dma_start(out=x_sb[0][:], in_=x[0])
-        nc.sync.dma_start(out=d_pad[0:KM, :], in_=D[:, :])
         nc.sync.dma_start(out=wb_sb[0][:, :, 0:128], in_=wb0[:, :, 0:128])
+        nc.sync.dma_start(out=d_pad[0:KM, :], in_=D[:, :])
         nc.sync.dma_start(out=wb_sb[0][:, :, 128:256], in_=wb0[:, :, 128:256])
         nc.sync.dma_start(out=wb_sb[0][:, :, 256:512], in_=wb0[:, :, 256:512])
         nc.sync.dma_start(out=x_sb[1][:], in_=x[1])
@@ -172,7 +172,7 @@ def tile_phydgalerkinconv_kernel(tc, x, wbases, bases, weights, D, out):
 
         def parts(n):
             if n == 0:
-                return [(0, 2), (2, 2), (4, 4)]
+                return [(0, 1), (1, 1), (2, 2), (4, 4)]
             return [(4, 4)] if n in HALF else [(4, 4), (0, 4)]
 
         def project(n):
@@ -214,7 +214,7 @@ def tile_phydgalerkinconv_kernel(tc, x, wbases, bases, weights, D, out):
                 in1=d_modes(n, P - share(n), P).unsqueeze(1).to_broadcast([P, 4, share(n), 4]),
                 op=MULT,
             )
-            for h, (first, count) in enumerate(parts(n)):
+            for h, (first, count) in sorted(enumerate(parts(n)), key=lambda part: part[1][0]):
                 width = P if first < 4 else P - share(n)
                 nc.vector.tensor_tensor(
                     out=zv[:, first:first + count, 0:width, :],
@@ -322,8 +322,8 @@ def tile_phydgalerkinconv_kernel(tc, x, wbases, bases, weights, D, out):
             [(scale_d, (3, 0))],
             [(scale_d, (3, 2))],
             [(turn_z, (3, 0)), (turn_z, (3, 1))],
+            [(transpose_weights, (3,))],
             [(transpose_bases, (0, 0))],
-            [(transpose_bases, (0, 3))],
             [],
         ]
         late_jobs = [
@@ -331,10 +331,10 @@ def tile_phydgalerkinconv_kernel(tc, x, wbases, bases, weights, D, out):
             [(replicate_d, (2,)), (replicate_d, (3,)), (transpose_d, (3,))],
             [(scale_d, (3, 1)), (transpose_weights, (0,))],
             [(scale_d, (3, 3)), (transpose_weights, (1,))],
-            [(transpose_weights, (2,)), (transpose_weights, (3,))],
-            [(transpose_bases, (0, 1)), (transpose_bases, (0, 2))],
-            [(transpose_bases, (1, 0)), (transpose_bases, (1, 1)), (contract, (0,))],
-            [(contract, (1,)), (contract, (2,)), (transpose_bases, (1, 2)), (transpose_bases, (1, 3)), (contract, (3,)), (round_y, (0, 0, 4)), (contract, (3 + 1,))],
+            [(transpose_weights, (2,))],
+            [],
+            [(transpose_bases, (0, 1)), (transpose_bases, (0, 2)), (transpose_bases, (0, 3)), (contract, (0,))],
+            [(transpose_bases, (1, 0)), (transpose_bases, (1, 1)), (contract, (1,)), (contract, (2,)), (transpose_bases, (1, 2)), (transpose_bases, (1, 3)), (contract, (3,)), (round_y, (0, 0, 4)), (contract, (4,))],
         ]
         quantises = [
             [],
@@ -357,8 +357,8 @@ def tile_phydgalerkinconv_kernel(tc, x, wbases, bases, weights, D, out):
         project(1)
         for r in range(NU):
             if r == 0:
-                spread(0, 1)
-                spread(0, 2)
+                for h in range(1, 4):
+                    spread(0, h)
             elif r not in HALF:
                 spread(r, 1)
             if r == 1:

from contextlib import ExitStack

import concourse.mybir as mybir
from concourse.masks import make_identity

F32 = mybir.dt.float32
BF16 = mybir.dt.bfloat16
U32 = mybir.dt.uint32
U8 = mybir.dt.uint8
FP8X4 = mybir.dt.float8_e4m3fn_x4
MULT = mybir.AluOpType.mult
COPY = mybir.ActivationFunctionType.Copy

NB, CI, CO, NPTS, KM, NM = 2, 128, 128, 1024, 32, 512
P = 128
NG = NPTS // P
NKC = NM // P
NC = CI * KM // 512
NU = NB * NKC
HALF = (NKC - 1,)
AG_FIRST, AG_HALF, AG = 56, 36, 76
FLOPS = 2 * NB * (CI * NPTS * NM + CI * KM * CO * NM + CO * NM * NPTS)


def tile_phydgalerkinconv_kernel(tc, x, wbases, bases, weights, D, out):
    nc = tc.nc
    with ExitStack() as ctx:
        keep = ctx.enter_context(tc.tile_pool(name="keep", bufs=1))
        work = ctx.enter_context(tc.tile_pool(name="work", bufs=2))
        psum = ctx.enter_context(tc.psum_pool(name="psum", bufs=2))
        ctx.enter_context(tc.manual_schedule())

        d_pad = keep.tile([P, NM], BF16, name="d_pad")
        ident_b = keep.tile([P, P], BF16, name="ident_b")
        make_identity(nc, ident_b[:])
        ident_f = keep.tile([P, P], F32, name="ident_f")
        make_identity(nc, ident_f[:])

        warm_in = keep.tile([P, 4 * P], BF16, name="warm_in", align_bytes=64)
        warm_code = keep.tile([P, P], U32, name="warm_code", align_bytes=64)
        warm_scale = keep.tile([P, P], U8, name="warm_scale", align_bytes=64)
        nc.vector.memset(warm_in[:].bitcast(F32), 0.0)
        nc.vector.quantize_mx(out=warm_code[:].bitcast(FP8X4), scales=warm_scale[:], in_=warm_in[:])
        nc.vector.memset(d_pad[32:64, :].bitcast(F32), 0.0)
        nc.vector.memset(d_pad[64:P, :].bitcast(F32), 0.0)
        warm_ps = psum.tile([P, P], F32, tag="xr", bufs=4, name="warm_ps")
        for w in range(12):
            nc.tensor.matmul_mx(
                out=warm_ps[:], lhsT=warm_code[:].bitcast(FP8X4), lhsT_scale=warm_scale[:],
                rhs=warm_code[:].bitcast(FP8X4), rhs_scale=warm_scale[:], start=True, stop=True,
            )

        x_sb = [keep.tile([P, NPTS], BF16, name="x_sb%d" % b) for b in range(NB)]
        wb_sb = [keep.tile([P, NG, NM], BF16, name="wb_sb%d" % b) for b in range(NB)]
        bs_sb = [keep.tile([P, NG * NM], BF16, name="bs_sb%d" % b) for b in range(NB)]
        w_om = keep.tile([P, CI * KM], BF16, name="w_om")

        wb0 = wbases[0].rearrange("(g p) k -> p g k", p=P)
        nc.sync.dma_start(out=x_sb[0][:], in_=x[0])
        nc.sync.dma_start(out=wb_sb[0][:, :, 0:128], in_=wb0[:, :, 0:128])
        nc.sync.dma_start(out=d_pad[0:KM, :], in_=D[:, :])
        nc.sync.dma_start(out=wb_sb[0][:, :, 128:256], in_=wb0[:, :, 128:256])
        nc.sync.dma_start(out=wb_sb[0][:, :, 256:512], in_=wb0[:, :, 256:512])
        nc.sync.dma_start(out=x_sb[1][:], in_=x[1])
        nc.sync.dma_start(out=wb_sb[1][:], in_=wbases[1].rearrange("(g p) k -> p g k", p=P))

        def load_bases(b):
            nc.sync.dma_start(
                out=bs_sb[b][:].rearrange("p (g k) -> p g k", g=NG),
                in_=bases[b].rearrange("(g p) k -> p g k", p=P),
            )

        for q in range(4):
            nc.sync.dma_start(
                out=w_om[:, 1024 * q:1024 * (q + 1)].rearrange("o (i j) -> o i j", j=KM),
                in_=weights[32 * q:32 * (q + 1)].rearrange("i o j -> o i j"),
            )
        load_bases(0)
        load_bases(1)

        x_t = [keep.tile([P, NG, CI], BF16, name="x_t%d" % b) for b in range(NB)]

        def transpose_x(b, half):
            xt_ps = psum.tile([P, 4, CI], BF16, tag="aux", name="xt_ps")
            for gg in range(4):
                g = 4 * half + gg
                nc.tensor.transpose(xt_ps[:, gg, :], x_sb[b][:, g * P:(g + 1) * P], ident_b[:])
            if b == 0:
                nc.vector.tensor_copy(out=x_t[b][:, 4 * half:4 * half + 4, :], in_=xt_ps[:])
            else:
                nc.scalar.copy(out=x_t[b][:, 4 * half:4 * half + 4, :], in_=xt_ps[:])

        selector = keep.tile([P, 4, P], BF16, name="selector")
        nc.vector.tensor_copy(
            out=selector[:].rearrange("j t (i r) -> j t i r", r=8),
            in_=ident_b[:, 0:KM].rearrange("j (r t) -> j t r", t=4).unsqueeze(2).to_broadcast([P, 4, 16, 8]),
        )
        d_rep = keep.tile([P, NM, 4], BF16, name="d_rep")

        def replicate_d(q):
            if q < 2:
                dr_ps = psum.tile([P, 4, P], F32, tag="xr", bufs=4, name="dr_ps")
            else:
                dr_ps = psum.tile([P, 4, P], F32, tag="aux", name="dr_ps")
            for t in range(4):
                nc.tensor.matmul(
                    out=dr_ps[:, t, :], lhsT=selector[:, t, :], rhs=d_pad[:, P * q:P * (q + 1)], start=True, stop=True,
                )
            copy = nc.vector.tensor_copy if q < 2 else nc.scalar.copy
            copy(out=d_rep[:, P * q:P * (q + 1), :], in_=dr_ps[:].rearrange("p t m -> p m t"))

        def d_modes(n, first, last):
            b, kc = divmod(n, NKC)
            if b == 0:
                return d_rep[:, P * kc + first:P * kc + last, :]
            return d_rep[:].rearrange("p (q e) t -> p e q t", e=NKC)[:, kc, first:last, :]

        w_grp = keep.tile([P, NC * CO * 4], BF16, name="w_grp", align_bytes=64)
        w_code = keep.tile([P, NC * CO], U32, name="w_code", align_bytes=64)
        w_scale = keep.tile([P, NC * CO], U8, name="w_scale", align_bytes=64)

        def turn_words(source, target, cp):
            words = source[:].bitcast(F32).rearrange("o (c p u) -> o c p u", p=P, u=2)
            grp_words = target[:].bitcast(F32).rearrange("p (c o u) -> p c o u", c=NC, u=2)
            wt_ps = psum.tile([P, 2, 2, CO], F32, tag="aux", name="wt_ps")
            for cc in range(2):
                for u in range(2):
                    nc.tensor.transpose(wt_ps[:, cc, u, :], words[:, 2 * cp + cc, :, u], ident_f[:])
            nc.scalar.copy(
                out=grp_words[:, 2 * cp:2 * cp + 2, :, :],
                in_=wt_ps[:].rearrange("p c u o -> p c o u"),
            )

        def transpose_weights(cp):
            turn_words(w_om, w_grp, cp)

        def quantise_weights():
            nc.vector.quantize_mx(out=w_code[:].bitcast(FP8X4), scales=w_scale[:], in_=w_grp[:])

        b_grp = [keep.tile([P, NPTS * 4], BF16, name="b_grp%d" % b, align_bytes=64) for b in range(NB)]
        b_code = [keep.tile([P, NPTS], U32, name="b_code%d" % b, align_bytes=64) for b in range(NB)]
        b_scale = [keep.tile([P, NPTS], U8, name="b_scale%d" % b, align_bytes=64) for b in range(NB)]

        def transpose_bases(b, gp):
            words = bs_sb[b][:].bitcast(F32).rearrange("p (g w u) -> p g u w", g=NG, u=2)
            grp_words = b_grp[b][:].bitcast(F32).rearrange("p (g n u) -> p g n u", g=NG, u=2)
            bt_ps = psum.tile([P, 2, 2, P], F32, tag="aux", name="bt_ps")
            for gg in range(2):
                for u in range(2):
                    nc.tensor.transpose(bt_ps[:, gg, u, :], words[:, 2 * gp + gg, u, :], ident_f[:])
            nc.scalar.copy(
                out=grp_words[:, 2 * gp:2 * gp + 2, :, :],
                in_=bt_ps[:].rearrange("p g u n -> p g n u"),
            )

        def quantise_bases(b, first, last):
            nc.vector.quantize_mx(
                out=b_code[b][:, first:last].bitcast(FP8X4), scales=b_scale[b][:, first:last], in_=b_grp[b][:, 4 * first:4 * last],
            )

        z_code = [keep.tile([P, NC * P], U32, name="z_code%d" % n, align_bytes=64) for n in range(NU)]
        z_scale = [keep.tile([P, NC * P], U8, name="z_scale%d" % n, align_bytes=64) for n in range(NU)]
        xh = {}
        rep = {}
        xr = {}
        xg = {}
        z = {}
        y_t = {}

        def share(n):
            return AG_FIRST if n == 0 else AG_HALF if n in HALF else AG

        def parts(n):
            if n == 0:
                return [(0, 1), (1, 1), (2, 2), (4, 4)]
            return [(4, 4)] if n in HALF else [(4, 4), (0, 4)]

        def project(n):
            b, kc = divmod(n, NKC)
            pattern = "p g (e q) -> p g e q" if b == 0 else "p g (q e) -> p g e q"
            wbv = wb_sb[b][:].rearrange(pattern, e=NKC)
            xh[n] = psum.tile([P, CI], F32, tag="acc", name="xh")
            for g in range(NG):
                nc.tensor.matmul(
                    out=xh[n][:], lhsT=wbv[:, g, kc, :], rhs=x_t[b][:, g, :],
                    start=(g == 0), stop=(g == NG - 1),
                )

        def replicate(n):
            rep[n] = work.tile([P, CI * 8], F32, tag="rep", bufs=3, name="rep")
            for c, count in parts(n):
                nc.scalar.copy(
                    out=rep[n][:, P * c:P * (c + count)].rearrange("k (i r) -> k i r", r=8),
                    in_=xh[n][:, 16 * c:16 * (c + count)].unsqueeze(2).to_broadcast([P, 16 * count, 8]),
                )

        def spread(n, h):
            first, count = parts(n)[h]
            xr[n, h] = psum.tile([P, count, P], F32, tag="xr", bufs=4, name="xr")
            for cc in range(count):
                c = first + cc
                nc.tensor.transpose(xr[n, h][:, cc, :], rep[n][:, c * P:(c + 1) * P], ident_f[:])
            if first == 4:
                xg[n] = work.tile([P, 4, share(n)], F32, tag="xg", bufs=3, name="xg")
                nc.scalar.copy(out=xg[n][:], in_=xr[n, h][:, :, P - share(n):P])

        def multiply(n):
            if n not in HALF:
                z[n] = work.tile([P, NC * P * 4], BF16, tag="z", name="z", align_bytes=64)
            zv = z[n][:].rearrange("p (c k t) -> p c k t", c=NC, t=4)
            nc.gpsimd.tensor_tensor(
                out=zv[:, 4:NC, P - share(n):P, :],
                in0=xg[n][:].unsqueeze(3).to_broadcast([P, 4, share(n), 4]),
                in1=d_modes(n, P - share(n), P).unsqueeze(1).to_broadcast([P, 4, share(n), 4]),
                op=MULT,
            )
            for h, (first, count) in sorted(enumerate(parts(n)), key=lambda part: part[1][0]):
                width = P if first < 4 else P - share(n)
                nc.vector.tensor_tensor(
                    out=zv[:, first:first + count, 0:width, :],
                    in0=xr[n, h][:, :, 0:width].unsqueeze(3).to_broadcast([P, count, width, 4]),
                    in1=d_modes(n, 0, width).unsqueeze(1).to_broadcast([P, count, width, 4]),
                    op=MULT,
                )

        d_t = {n: keep.tile([P, KM], BF16, name="d_t%d" % n) for n in HALF}
        x_half = {n: keep.tile([P, CI // 2], F32, name="x_half%d" % n) for n in HALF}
        for n in HALF:
            z[n] = keep.tile([P, NC * P * 4], BF16, name="z_half%d" % n, align_bytes=64)
        z_km = {n: keep.tile([P, CI // 2 * KM], BF16, name="z_km%d" % n) for n in HALF}

        def transpose_d(n):
            b, kc = divmod(n, NKC)
            modes = d_pad[:, P * kc:P * (kc + 1)] if b == 0 else d_pad[:, kc:NM:NKC]
            dt_ps = psum.tile([P, P], BF16, tag="aux", name="dt_ps")
            nc.tensor.transpose(dt_ps[:], modes, ident_b[:])
            nc.scalar.copy(out=d_t[n][:], in_=dt_ps[:, 0:KM])

        def keep_x(n):
            nc.scalar.copy(out=x_half[n][:], in_=xh[n][:, 0:CI // 2])

        def scale_d(n, part):
            for i in range(16 * part, 16 * (part + 1)):
                nc.scalar.activation(
                    out=z_km[n][:, KM * i:KM * (i + 1)], in_=d_t[n][:], func=COPY, scale=x_half[n][:, i:i + 1],
                )

        def turn_z(n, cp):
            turn_words(z_km[n], z[n], cp)

        def quantise(n, pieces):
            wide = NC * P // pieces
            for s in range(pieces):
                nc.vector.quantize_mx(
                    out=z_code[n][:, wide * s:wide * (s + 1)].bitcast(FP8X4),
                    scales=z_scale[n][:, wide * s:wide * (s + 1)],
                    in_=z[n][:, 4 * wide * s:4 * wide * (s + 1)],
                )

        def contract(n):
            b, kc = divmod(n, NKC)
            if kc == 0:
                y_t[b] = psum.tile([P, NKC, CO], F32, tag="acc", name="y_t")
            for c in range(NC):
                z_op = z_code[n][:, c * P:(c + 1) * P].bitcast(FP8X4), z_scale[n][:, c * P:(c + 1) * P]
                w_op = w_code[:, c * CO:(c + 1) * CO].bitcast(FP8X4), w_scale[:, c * CO:(c + 1) * CO]
                stationary, moving = (w_op, z_op) if b == 0 else (z_op, w_op)
                nc.tensor.matmul_mx(
                    out=y_t[b][:, kc, :],
                    lhsT=stationary[0], lhsT_scale=stationary[1], rhs=moving[0], rhs_scale=moving[1],
                    start=(c == 0), stop=(c == NC - 1),
                )

        y_om = keep.tile([P, NM], BF16, name="y_om", align_bytes=64)
        yg = {}
        yc = {}
        ys = {}

        def round_y(b, first, last):
            if first == 0:
                yg[b] = work.tile([P, CO * 4], BF16, tag="yg", name="yg", align_bytes=64)
            if b == 0:
                nc.scalar.copy(out=y_om[:], in_=y_t[b][:].rearrange("o e m -> o (e m)"))
            else:
                nc.scalar.copy(
                    out=yg[b][:].rearrange("p (o t) -> p o t", t=4)[:, :, first:last],
                    in_=y_t[b][:, first:last, :].rearrange("p t o -> p o t"),
                )

        def turn_y(b):
            words = y_om[:].bitcast(F32).rearrange("o (p u) -> o p u", u=2)
            yt_ps = psum.tile([P, 2, CO], F32, tag="aux", name="yt_ps")
            for u in range(2):
                nc.tensor.transpose(yt_ps[:, u, :], words[:, :, u], ident_f[:])
            nc.scalar.copy(
                out=yg[b][:].bitcast(F32).rearrange("p (o u) -> p o u", u=2), in_=yt_ps[:].rearrange("p u o -> p o u"),
            )

        def quantise_y(b):
            yc[b] = work.tile([P, CO], U32, tag="yc", name="yc", align_bytes=64)
            ys[b] = work.tile([P, CO], U8, tag="ys", name="ys", align_bytes=64)
            nc.vector.quantize_mx(out=yc[b][:].bitcast(FP8X4), scales=ys[b][:], in_=yg[b][:])

        def reconstruct(b, nh):
            yo = work.tile([P, 512], F32, tag="yo", bufs=4, name="yo")
            copies = [nc.vector.tensor_copy, nc.scalar.copy] if b == NB - 1 and nh == 1 else [nc.scalar.copy]
            wide = 512 // len(copies)
            for piece, copy in enumerate(copies):
                first = 512 * nh + wide * piece
                yp = psum.tile([P, wide], F32, tag="xr", bufs=4, name="yp")
                nc.tensor.matmul_mx(
                    out=yp[:], lhsT=yc[b][:].bitcast(FP8X4), lhsT_scale=ys[b][:],
                    rhs=b_code[b][:, first:first + wide].bitcast(FP8X4), rhs_scale=b_scale[b][:, first:first + wide],
                    start=True, stop=True,
                )
                copy(out=yo[:, wide * piece:wide * (piece + 1)], in_=yp[:])
            nc.sync.dma_start(out=out[b][:, 512 * nh:512 * (nh + 1)], in_=yo[:])

        early_jobs = [
            [],
            [],
            [(scale_d, (3, 0))],
            [(scale_d, (3, 2))],
            [(turn_z, (3, 0)), (turn_z, (3, 1))],
            [(transpose_weights, (3,))],
            [(transpose_bases, (0, 0))],
            [],
        ]
        late_jobs = [
            [],
            [(replicate_d, (2,)), (replicate_d, (3,)), (transpose_d, (3,))],
            [(scale_d, (3, 1)), (transpose_weights, (0,))],
            [(scale_d, (3, 3)), (transpose_weights, (1,))],
            [(transpose_weights, (2,))],
            [],
            [(transpose_bases, (0, 1)), (transpose_bases, (0, 2)), (transpose_bases, (0, 3)), (contract, (0,))],
            [(transpose_bases, (1, 0)), (transpose_bases, (1, 1)), (contract, (1,)), (contract, (2,)), (transpose_bases, (1, 2)), (transpose_bases, (1, 3)), (contract, (3,)), (round_y, (0, 0, 4)), (contract, (4,))],
        ]
        quantises = [
            [],
            [(quantise, (0, 1))],
            [],
            [(quantise, (1, 1))],
            [(quantise, (2, 1))],
            [(quantise_weights, ()), (quantise, (3, 1)), (quantise, (4, 1))],
            [(quantise, (5, 1))],
            [(quantise, (6, 1))],
        ]

        transpose_x(0, 0)
        transpose_x(0, 1)
        replicate_d(0)
        replicate_d(1)
        project(0)
        replicate(0)
        spread(0, 0)
        project(1)
        for r in range(NU):
            if r == 0:
                for h in range(1, 4):
                    spread(0, h)
            elif r not in HALF:
                spread(r, 1)
            if r == 1:
                transpose_x(1, 0)
                transpose_x(1, 1)
            if r + 2 < NU:
                project(r + 2)
            if r + 1 < NU:
                replicate(r + 1)
            if r + 1 in HALF:
                keep_x(r + 1)
            for job, arguments in early_jobs[r]:
                job(*arguments)
            if r + 1 < NU:
                spread(r + 1, 0)
            for job, arguments in late_jobs[r]:
                job(*arguments)
            multiply(r)
            for job, arguments in quantises[r]:
                job(*arguments)
        turn_y(0)
        contract(NU - 3)
        round_y(1, 0, 2)
        contract(NU - 2)
        quantise_bases(0, 0, 512)
        quantise_y(0)
        reconstruct(0, 0)
        quantise(NU - 1, 4)
        contract(NU - 1)
        round_y(1, 2, 4)
        quantise_bases(0, 512, NPTS)
        reconstruct(0, 1)
        quantise_bases(1, 0, 512)
        quantise_y(1)
        reconstruct(1, 0)
        quantise_bases(1, 512, NPTS)
        reconstruct(1, 1)
